import numpy as np
import ml_dtypes


def mxq(x, axis, fmt="e4m3"):
    dtype, down = {"e4m3": (ml_dtypes.float8_e4m3fn, 7), "e5m2": (ml_dtypes.float8_e5m2, 14)}[fmt]
    v = np.moveaxis(np.asarray(x, np.float32).astype(ml_dtypes.bfloat16).astype(np.float64), axis, -1)
    blocks = v.reshape(v.shape[:-1] + (-1, 32))
    amax = np.abs(blocks).max(-1, keepdims=True)
    byte = np.maximum(np.where(amax > 0, np.frexp(amax)[1] - 1 + 127, 0) - down, 1)
    scale = np.exp2(byte - 127.0)
    codes = (blocks / scale).astype(np.float32).astype(dtype).astype(np.float64)
    return np.moveaxis((codes * scale).reshape(v.shape), -1, axis)


WIDE = False


def mx_kscale(k):
    if not WIDE:
        return np.ones(k)
    levels = np.array([10, -10, 5, -5, 0])
    a = np.random.permutation(np.resize(levels, k // 512 * 4)).reshape(k // 512, 4)
    idx = np.arange(k)
    return np.exp2(a[idx // 512, idx % 128 // 32])


BF16 = ml_dtypes.bfloat16


def bf(x):
    return np.asarray(x, np.float32).astype(BF16)


def f64(x):
    return np.asarray(x).astype(np.float64)


E2M1 = np.array([0.0, 0.5, 1.0, 1.5, 2.0, 3.0, 4.0, 6.0, -0.0, -0.5, -1.0, -1.5, -2.0, -3.0, -4.0, -6.0])


def pack_weight(w, fmt):
    k, n = w.shape
    w = f64(bf(w)).reshape(k // 32, 32, n)
    amax = np.abs(w).max(1)
    if fmt == "e4m3":
        byte = np.frexp(amax)[1] - 1 + 127 - 7
    else:
        mant, ex = np.frexp(amax / 6.0)
        byte = np.where(mant > 0.5, ex, ex - 1) + 127
    byte = np.clip(np.where(amax > 0, byte, 1), 1, 254)
    scaled = (w * np.exp2(127.0 - byte)[:, None, :]).reshape(k, n).astype(np.float32)
    by_word = np.ascontiguousarray(scaled.reshape(k // 512, 128, 4, n).transpose(0, 1, 3, 2))
    if fmt == "e4m3":
        words = by_word.astype(ml_dtypes.float8_e4m3fn).view(np.uint8)
    else:
        c = by_word.astype(ml_dtypes.float4_e2m1fn).view(np.uint8) & 0xF
        words = c[..., 0::2] | (c[..., 1::2] << 4)
    return np.ascontiguousarray(words), np.ascontiguousarray(byte.astype(np.uint8).reshape(k // 512, 16, n))


def unpack_weight(words, scales, fmt):
    g, p, n, _ = words.shape
    if fmt == "e4m3":
        vals = np.ascontiguousarray(words).view(ml_dtypes.float8_e4m3fn).astype(np.float64)
    else:
        nib = np.empty((g, p, n, 4), np.uint8)
        nib[..., 0::2] = words & 0xF
        nib[..., 1::2] = words >> 4
        vals = E2M1[nib]
    vals = vals * np.repeat(np.exp2(scales.astype(np.float64) - 127.0), 8, axis=1)[..., None]
    return vals.transpose(0, 1, 3, 2).reshape(g * 512, n)


BS, H, XDIM = 1024, 512, 1024
IN = XDIM + 2 * H
FMT = "e4m3"


def sigmoid(v):
    return 1.0 / (1.0 + np.exp(-v))


def setup_inputs():
    s = mx_kscale(IN)
    c = 1.0 / np.sqrt(IN)

    def draw_w():
        return pack_weight((np.random.standard_normal((H, IN)) * c / s[None, :]).T, FMT)

    def draw_b():
        return bf(np.random.standard_normal(H) * 0.3)

    input_x = bf(np.random.standard_normal((BS, XDIM)) * s[:XDIM])
    previous_time = bf(np.random.standard_normal((BS, H)) * s[XDIM:XDIM + H])
    previous_layer = bf(np.random.standard_normal((BS, H)) * s[XDIM + H:])
    old_state = bf(np.random.standard_normal((BS, H)) * 0.5)
    wi_words, wi_scales = draw_w()
    b_i = draw_b()
    wf_words, wf_scales = draw_w()
    b_f = draw_b()
    wo_words, wo_scales = draw_w()
    b_o = draw_b()
    ws_words, ws_scales = draw_w()
    b_s = draw_b()
    return {
        "input_x": input_x,
        "previous_time": previous_time,
        "previous_layer": previous_layer,
        "old_state": old_state,
        "Wi_words": wi_words, "Wi_scales": wi_scales, "bi": b_i,
        "Wf_words": wf_words, "Wf_scales": wf_scales, "bf": b_f,
        "Wo_words": wo_words, "Wo_scales": wo_scales, "bo": b_o,
        "Ws_words": ws_words, "Ws_scales": ws_scales, "bs_state": b_s,
    }


def reference(input_x, previous_time, previous_layer, old_state, Wi_words, Wi_scales, bi, Wf_words, Wf_scales, bf, Wo_words, Wo_scales, bo, Ws_words, Ws_scales, bs_state):
    z = np.concatenate([f64(input_x), f64(previous_time), f64(previous_layer)], axis=1)
    W_all_t = np.concatenate([
        unpack_weight(Wi_words, Wi_scales, FMT),
        unpack_weight(Wf_words, Wf_scales, FMT),
        unpack_weight(Wo_words, Wo_scales, FMT),
        unpack_weight(Ws_words, Ws_scales, FMT),
    ], axis=1)
    b_all = np.concatenate([f64(bi), f64(bf), f64(bo), f64(bs_state)], axis=0)
    proj = (mxq(z, 1, "e4m3") @ W_all_t) + b_all
    gi, gf, go, gs = np.split(proj, 4, axis=1)
    input_gate = sigmoid(gi)
    forget_gate = sigmoid(gf)
    output_gate = sigmoid(go)
    new_state = forget_gate * f64(old_state) + input_gate * np.tanh(gs)
    new_hidden = output_gate * np.tanh(new_state)
    return new_hidden

@@ -1,0 +1,223 @@
+import concourse.mybir as mybir
+from concourse.masks import make_identity
+
+F32 = mybir.dt.float32
+BF16 = mybir.dt.bfloat16
+I32 = mybir.dt.int32
+U32 = mybir.dt.uint32
+U8 = mybir.dt.uint8
+FP8X4 = mybir.dt.float8_e4m3fn_x4
+ACT = mybir.ActivationFunctionType
+
+P = 128
+PACK = 4
+K_PASS = P * PACK
+BATCH = 1024
+HID = 512
+K = 2048
+PASSES = K // K_PASS
+ROW_TILES = BATCH // P
+PAIR = 2
+PAIRS = ROW_TILES // PAIR
+BANKS = 8
+
+BLOCKS = ROW_TILES * PASSES
+LOAD_BLOCKS = 4
+LOADS = BLOCKS // LOAD_BLOCKS
+PAIR_WORDS = K_PASS // 2
+
+FORGET, CANDIDATE, INPUT, OUTPUT = 0, 1, 2, 3
+GATES = 4
+
+FLOPS = 2 * BATCH * K * GATES * HID
+
+
+def tile_rnn_unit_kernel(
+    tc,
+    input_x,
+    previous_time,
+    previous_layer,
+    old_state,
+    Wi_words,
+    Wi_scales,
+    bi,
+    Wf_words,
+    Wf_scales,
+    bf,
+    Wo_words,
+    Wo_scales,
+    bo,
+    Ws_words,
+    Ws_scales,
+    bs_state,
+    out,
+):
+    nc = tc.nc
+    gates = (
+        (Wf_words, Wf_scales, bf, ACT.Sigmoid),
+        (Ws_words, Ws_scales, bs_state, ACT.Tanh),
+        (Wi_words, Wi_scales, bi, ACT.Sigmoid),
+        (Wo_words, Wo_scales, bo, ACT.Sigmoid),
+    )
+    z_parts = ((input_x, 0), (previous_time, 2), (previous_layer, 3))
+
+    with (
+        tc.tile_pool(name="resident", bufs=1) as resident,
+        tc.tile_pool(name="stage", bufs=3) as stage,
+        tc.psum_pool(name="psum", bufs=BANKS) as psum,
+        tc.manual_schedule(),
+    ):
+        bias_rows = resident.tile([P, GATES, HID], BF16)
+        nc.vector.memset(bias_rows[:], 0.0)
+        ones = resident.tile([P, P], BF16)
+        nc.vector.memset(ones[:], 1.0)
+        for gate in range(GATES):
+            nc.scalar.dma_start(
+                out=bias_rows[0:1, gate, :],
+                in_=gates[gate][2].rearrange("(o n) -> o n", o=1),
+            )
+        w_planes = resident.tile([P, GATES, HID], U8, align_bytes=64)
+        nc.vector.memset(w_planes[:].rearrange("p w n -> p (w n)").bitcast(I32), 0)
+        identity = resident.tile([P, P], F32)
+        make_identity(nc, identity[:])
+
+        z_raw = resident.tile([P, LOADS, LOAD_BLOCKS * K_PASS], BF16)
+        block_of = {}
+        for part, first_pass in z_parts:
+            passes_here = part.shape[1] // K_PASS
+            flat = part.rearrange("(p m) k -> p (m k)", m=ROW_TILES)
+            for n in range(ROW_TILES * passes_here):
+                block = len(block_of)
+                block_of[(n // passes_here, first_pass + n % passes_here)] = block
+                if n % LOAD_BLOCKS == 0:
+                    nc.sync.dma_start(
+                        out=z_raw[:, block // LOAD_BLOCKS, :],
+                        in_=flat[:, n * K_PASS : (n + LOAD_BLOCKS) * K_PASS],
+                    )
+        w_words = resident.tile([P, GATES, PASSES, HID], I32, align_bytes=64)
+        old_rows = resident.tile([P, ROW_TILES, HID], BF16)
+        for gate in range(GATES):
+            words, scales = gates[gate][0], gates[gate][1]
+            for quadrant in range(4):
+                nc.sync.dma_start(
+                    out=w_planes[32 * quadrant : 32 * quadrant + 16, gate, :].bitcast(I32),
+                    in_=scales[:, 4 * quadrant : 4 * quadrant + 4, :].bitcast(I32),
+                )
+            for g in range(PASSES):
+                nc.sync.dma_start(
+                    out=w_words[:, gate, g, :],
+                    in_=words[g].rearrange("p n t -> p (n t)").bitcast(I32),
+                )
+            if gate == FORGET:
+                nc.sync.dma_start(
+                    out=old_rows[:],
+                    in_=old_state.rearrange("(p m) h -> p m h", m=ROW_TILES),
+                )
+
+        bias_all = resident.tile([P, GATES, HID], F32)
+        for gate in range(GATES):
+            spread = psum.tile([P, HID], F32, tag="bank")
+            nc.tensor.matmul(
+                out=spread[:], lhsT=ones[:], rhs=bias_rows[:, gate, :], start=True, stop=True
+            )
+            nc.scalar.copy(out=bias_all[:, gate, :], in_=spread[:])
+
+        z_codes = resident.tile([P, BLOCKS, P], U32, align_bytes=64)
+        z_planes = resident.tile([P, BLOCKS, P], U8, align_bytes=64)
+
+        def quantise(load, grouped):
+            blocks = slice(load * LOAD_BLOCKS, (load + 1) * LOAD_BLOCKS)
+            nc.vector.quantize_mx(
+                out=z_codes[:, blocks, :].rearrange("p b r -> p (b r)").bitcast(FP8X4),
+                scales=z_planes[:, blocks, :].rearrange("p b r -> p (b r)"),
+                in_=grouped[:].rearrange("p b r t -> p (b r t)"),
+            )
+
+        copied = None
+        for load in range(LOADS):
+            pair_words = z_raw[:, load, :].bitcast(F32)
+            grouped = stage.tile([P, LOAD_BLOCKS, P, PACK], BF16, align_bytes=64)
+            grouped_words = grouped[:].bitcast(F32)
+            for half in range(2):
+                turned = psum.tile([P, 2, 2, P], F32, tag="bank")
+                for b in range(2):
+                    first_word = (2 * half + b) * PAIR_WORDS
+                    for u in range(2):
+                        nc.tensor.transpose(
+                            turned[:, b, u, :],
+                            pair_words[:, first_word + u : first_word + PAIR_WORDS : 2],
+                            identity[:],
+                        )
+                side_by_side = turned[:].rearrange("p b u r -> p b r u")
+                if half == 0:
+                    nc.scalar.copy(out=grouped_words[:, 0:2, :, :], in_=side_by_side)
+                else:
+                    nc.vector.tensor_copy(out=grouped_words[:, 2:4, :, :], in_=side_by_side)
+            if copied is not None:
+                quantise(*copied)
+            copied = (load, grouped)
+        quantise(*copied)
+
+        values = resident.tile([P, GATES, ROW_TILES, HID], F32)
+        out_rows = out.rearrange("(p m) h -> p m h", m=ROW_TILES)
+
+        def project(gate, pair):
+            sums = [
+                psum.tile([P, HID], F32, tag="bank", name="sums%d" % i) for i in range(PAIR)
+            ]
+            for g in range(PASSES):
+                for i in range(PAIR):
+                    block = block_of[(PAIR * pair + i, g)]
+                    nc.tensor.matmul_mx(
+                        out=sums[i][:],
+                        lhsT=z_codes[:, block, :].bitcast(FP8X4),
+                        lhsT_scale=z_planes[:, block, :],
+                        rhs=w_words[:, gate, g, :].bitcast(FP8X4),
+                        rhs_scale=w_planes[PACK * g : P, gate, :],
+                        start=(g == 0),
+                        stop=(g == PASSES - 1),
+                    )
+            for i in range(PAIR):
+                gate_rows = values[:, gate, PAIR * pair + i, :]
+                nc.vector.tensor_add(out=gate_rows, in0=sums[i][:], in1=bias_all[:, gate, :])
+                nc.scalar.activation(out=gate_rows, in_=gate_rows, func=gates[gate][3])
+
+        def combine(gate, pair):
+            for i, engine in enumerate((nc.gpsimd, nc.vector)):
+                m = PAIR * pair + i
+                if gate == FORGET:
+                    engine.tensor_mul(
+                        out=values[:, FORGET, m, :],
+                        in0=values[:, FORGET, m, :],
+                        in1=old_rows[:, m, :],
+                    )
+                if gate == INPUT:
+                    engine.tensor_mul(
+                        out=values[:, INPUT, m, :],
+                        in0=values[:, INPUT, m, :],
+                        in1=values[:, CANDIDATE, m, :],
+                    )
+                    engine.tensor_add(
+                        out=values[:, INPUT, m, :],
+                        in0=values[:, INPUT, m, :],
+                        in1=values[:, FORGET, m, :],
+                    )
+                    nc.scalar.activation(
+                        out=values[:, INPUT, m, :], in_=values[:, INPUT, m, :], func=ACT.Tanh
+                    )
+                if gate == OUTPUT:
+                    engine.tensor_mul(
+                        out=values[:, OUTPUT, m, :],
+                        in0=values[:, OUTPUT, m, :],
+                        in1=values[:, INPUT, m, :],
+                    )
+                    nc.sync.dma_start(out=out_rows[:, m, :], in_=values[:, OUTPUT, m, :])
+
+        projected = None
+        for gate in range(GATES):
+            for pair in range(PAIRS):
+                project(gate, pair)
+                if projected is not None:
+                    combine(*projected)
+                projected = (gate, pair)
+        combine(*projected)

@@ -68,14 +68,16 @@ def tile_rnn_unit_kernel(
         tc.manual_schedule(),
     ):
         bias_rows = resident.tile([P, GATES, HID], BF16)
-        nc.vector.memset(bias_rows[:], 0.0)
+        nc.vector.memset(bias_rows[:].rearrange("p w n -> p (w n)").bitcast(I32), 0)
         ones = resident.tile([P, P], BF16)
         nc.vector.memset(ones[:], 1.0)
         for gate in range(GATES):
-            nc.scalar.dma_start(
+            nc.sync.dma_start(
                 out=bias_rows[0:1, gate, :],
                 in_=gates[gate][2].rearrange("(o n) -> o n", o=1),
             )
+        warm = resident.tile([P, 1], F32)
+        nc.scalar.activation(out=warm[:], in_=ones[:, 0:1], func=ACT.Sigmoid)
         w_planes = resident.tile([P, GATES, HID], U8, align_bytes=64)
         nc.vector.memset(w_planes[:].rearrange("p w n -> p (w n)").bitcast(I32), 0)
         identity = resident.tile([P, P], F32)
@@ -213,11 +215,14 @@ def tile_rnn_unit_kernel(
                     )
                     nc.sync.dma_start(out=out_rows[:, m, :], in_=values[:, OUTPUT, m, :])
 
+        steps = [(FORGET, pair) for pair in range(PAIRS)]
+        for pair in range(PAIRS):
+            steps.extend([(CANDIDATE, pair), (INPUT, pair)])
+        steps.extend([(OUTPUT, pair) for pair in range(PAIRS)])
         projected = None
-        for gate in range(GATES):
-            for pair in range(PAIRS):
-                project(gate, pair)
-                if projected is not None:
-                    combine(*projected)
-                projected = (gate, pair)
+        for step in steps:
+            project(*step)
+            if projected is not None:
+                combine(*projected)
+            projected = step
         combine(*projected)

@@ -67,19 +67,21 @@ def tile_rnn_unit_kernel(
         tc.psum_pool(name="psum", bufs=BANKS) as psum,
         tc.manual_schedule(),
     ):
+        bias_line = resident.tile([1, GATES, HID], BF16)
+        for gate in range(GATES):
+            nc.sync.dma_start(
+                out=bias_line[0:1, gate, :],
+                in_=gates[gate][2].rearrange("(o n) -> o n", o=1),
+            )
         bias_rows = resident.tile([P, GATES, HID], BF16)
         nc.vector.memset(bias_rows[:].rearrange("p w n -> p (w n)").bitcast(I32), 0)
         ones = resident.tile([P, P], BF16)
         nc.vector.memset(ones[:], 1.0)
-        for gate in range(GATES):
-            nc.sync.dma_start(
-                out=bias_rows[0:1, gate, :],
-                in_=gates[gate][2].rearrange("(o n) -> o n", o=1),
-            )
         warm = resident.tile([P, 1], F32)
         nc.scalar.activation(out=warm[:], in_=ones[:, 0:1], func=ACT.Sigmoid)
         w_planes = resident.tile([P, GATES, HID], U8, align_bytes=64)
         nc.vector.memset(w_planes[:].rearrange("p w n -> p (w n)").bitcast(I32), 0)
+        nc.vector.tensor_copy(out=bias_rows[0:1, :, :], in_=bias_line[:])
         identity = resident.tile([P, P], F32)
         make_identity(nc, identity[:])
 
@@ -163,9 +165,10 @@ def tile_rnn_unit_kernel(
         values = resident.tile([P, GATES, ROW_TILES, HID], F32)
         out_rows = out.rearrange("(p m) h -> p m h", m=ROW_TILES)
 
-        def project(gate, pair):
+        def project(gate, pair, first, width):
+            cols = slice(first, first + width)
             sums = [
-                psum.tile([P, HID], F32, tag="bank", name="sums%d" % i) for i in range(PAIR)
+                psum.tile([P, width], F32, tag="bank", name="sums%d" % i) for i in range(PAIR)
             ]
             for g in range(PASSES):
                 for i in range(PAIR):
@@ -174,51 +177,54 @@ def tile_rnn_unit_kernel(
                         out=sums[i][:],
                         lhsT=z_codes[:, block, :].bitcast(FP8X4),
                         lhsT_scale=z_planes[:, block, :],
-                        rhs=w_words[:, gate, g, :].bitcast(FP8X4),
-                        rhs_scale=w_planes[PACK * g : P, gate, :],
+                        rhs=w_words[:, gate, g, cols].bitcast(FP8X4),
+                        rhs_scale=w_planes[PACK * g : P, gate, cols],
                         start=(g == 0),
                         stop=(g == PASSES - 1),
                     )
             for i in range(PAIR):
-                gate_rows = values[:, gate, PAIR * pair + i, :]
-                nc.vector.tensor_add(out=gate_rows, in0=sums[i][:], in1=bias_all[:, gate, :])
+                gate_rows = values[:, gate, PAIR * pair + i, cols]
+                nc.vector.tensor_add(out=gate_rows, in0=sums[i][:], in1=bias_all[:, gate, cols])
                 nc.scalar.activation(out=gate_rows, in_=gate_rows, func=gates[gate][3])
 
-        def combine(gate, pair):
+        def combine(gate, pair, first, width):
+            cols = slice(first, first + width)
             for i, engine in enumerate((nc.gpsimd, nc.vector)):
                 m = PAIR * pair + i
                 if gate == FORGET:
                     engine.tensor_mul(
-                        out=values[:, FORGET, m, :],
-                        in0=values[:, FORGET, m, :],
-                        in1=old_rows[:, m, :],
+                        out=values[:, FORGET, m, cols],
+                        in0=values[:, FORGET, m, cols],
+                        in1=old_rows[:, m, cols],
                     )
                 if gate == INPUT:
                     engine.tensor_mul(
-                        out=values[:, INPUT, m, :],
-                        in0=values[:, INPUT, m, :],
-                        in1=values[:, CANDIDATE, m, :],
+                        out=values[:, INPUT, m, cols],
+                        in0=values[:, INPUT, m, cols],
+                        in1=values[:, CANDIDATE, m, cols],
                     )
                     engine.tensor_add(
-                        out=values[:, INPUT, m, :],
-                        in0=values[:, INPUT, m, :],
-                        in1=values[:, FORGET, m, :],
+                        out=values[:, INPUT, m, cols],
+                        in0=values[:, INPUT, m, cols],
+                        in1=values[:, FORGET, m, cols],
                     )
                     nc.scalar.activation(
-                        out=values[:, INPUT, m, :], in_=values[:, INPUT, m, :], func=ACT.Tanh
+                        out=values[:, INPUT, m, cols], in_=values[:, INPUT, m, cols], func=ACT.Tanh
                     )
                 if gate == OUTPUT:
                     engine.tensor_mul(
-                        out=values[:, OUTPUT, m, :],
-                        in0=values[:, OUTPUT, m, :],
-                        in1=values[:, INPUT, m, :],
+                        out=values[:, OUTPUT, m, cols],
+                        in0=values[:, OUTPUT, m, cols],
+                        in1=values[:, INPUT, m, cols],
                     )
-                    nc.sync.dma_start(out=out_rows[:, m, :], in_=values[:, OUTPUT, m, :])
+                    nc.sync.dma_start(out=out_rows[:, m, cols], in_=values[:, OUTPUT, m, cols])
 
-        steps = [(FORGET, pair) for pair in range(PAIRS)]
+        steps = [(FORGET, pair, 0, HID) for pair in range(PAIRS)]
         for pair in range(PAIRS):
-            steps.extend([(CANDIDATE, pair), (INPUT, pair)])
-        steps.extend([(OUTPUT, pair) for pair in range(PAIRS)])
+            steps.extend([(CANDIDATE, pair, 0, HID), (INPUT, pair, 0, HID)])
+        steps.extend([(OUTPUT, pair, 0, HID) for pair in range(PAIRS - 1)])
+        half = HID // 2
+        steps.extend([(OUTPUT, PAIRS - 1, first, half) for first in (0, half)])
         projected = None
         for step in steps:
             project(*step)

@@ -32,6 +32,13 @@ GATES = 4
 FLOPS = 2 * BATCH * K * GATES * HID
 
 
+def block_of(m, g):
+    pair, i = m // PAIR, m % PAIR
+    if g < 2:
+        return LOAD_BLOCKS * (2 * pair) + 2 * i + g
+    return LOAD_BLOCKS * (2 * pair + 1) + 2 * (g - 2) + i
+
+
 def tile_rnn_unit_kernel(
     tc,
     input_x,
@@ -59,7 +66,6 @@ def tile_rnn_unit_kernel(
         (Wi_words, Wi_scales, bi, ACT.Sigmoid),
         (Wo_words, Wo_scales, bo, ACT.Sigmoid),
     )
-    z_parts = ((input_x, 0), (previous_time, 2), (previous_layer, 3))
 
     with (
         tc.tile_pool(name="resident", bufs=1) as resident,
@@ -86,21 +92,33 @@ def tile_rnn_unit_kernel(
         make_identity(nc, identity[:])
 
         z_raw = resident.tile([P, LOADS, LOAD_BLOCKS * K_PASS], BF16)
-        block_of = {}
-        for part, first_pass in z_parts:
-            passes_here = part.shape[1] // K_PASS
-            flat = part.rearrange("(p m) k -> p (m k)", m=ROW_TILES)
-            for n in range(ROW_TILES * passes_here):
-                block = len(block_of)
-                block_of[(n // passes_here, first_pass + n % passes_here)] = block
-                if n % LOAD_BLOCKS == 0:
-                    nc.sync.dma_start(
-                        out=z_raw[:, block // LOAD_BLOCKS, :],
-                        in_=flat[:, n * K_PASS : (n + LOAD_BLOCKS) * K_PASS],
-                    )
         w_words = resident.tile([P, GATES, PASSES, HID], I32, align_bytes=64)
         old_rows = resident.tile([P, ROW_TILES, HID], BF16)
-        for gate in range(GATES):
+        x_flat = input_x.rearrange("(p m) k -> p (m k)", m=ROW_TILES)
+        time_flat = previous_time.rearrange("(p m) k -> p (m k)", m=ROW_TILES)
+        layer_flat = previous_layer.rearrange("(p m) k -> p (m k)", m=ROW_TILES)
+        old_view = old_state.rearrange("(p m) h -> p m h", m=ROW_TILES)
+
+        def load_z(pair, pieces):
+            width = LOAD_BLOCKS * K_PASS // pieces
+            for piece in range(pieces):
+                nc.sync.dma_start(
+                    out=z_raw[:, 2 * pair, piece * width : (piece + 1) * width],
+                    in_=x_flat[
+                        :,
+                        pair * LOAD_BLOCKS * K_PASS
+                        + piece * width : pair * LOAD_BLOCKS * K_PASS
+                        + (piece + 1) * width,
+                    ],
+                )
+            half = PAIR * K_PASS
+            for n, flat in enumerate((time_flat, layer_flat)):
+                nc.sync.dma_start(
+                    out=z_raw[:, 2 * pair + 1, n * half : (n + 1) * half],
+                    in_=flat[:, pair * half : (pair + 1) * half],
+                )
+
+        def load_weight(gate):
             words, scales = gates[gate][0], gates[gate][1]
             for quadrant in range(4):
                 nc.sync.dma_start(
@@ -112,38 +130,44 @@ def tile_rnn_unit_kernel(
                     out=w_words[:, gate, g, :],
                     in_=words[g].rearrange("p n t -> p (n t)").bitcast(I32),
                 )
-            if gate == FORGET:
-                nc.sync.dma_start(
-                    out=old_rows[:],
-                    in_=old_state.rearrange("(p m) h -> p m h", m=ROW_TILES),
-                )
+
+        def load_old(pair):
+            rows = slice(PAIR * pair, PAIR * (pair + 1))
+            nc.sync.dma_start(out=old_rows[:, rows, :], in_=old_view[:, rows, :])
+
+        load_z(0, 2)
+        load_z(1, 1)
+        load_weight(FORGET)
+        load_z(2, 1)
+        load_old(0)
+        load_z(3, 1)
+        load_old(1)
+        load_old(2)
+        load_old(3)
+        load_weight(CANDIDATE)
+        load_weight(INPUT)
+        load_weight(OUTPUT)
 
         bias_all = resident.tile([P, GATES, HID], F32)
-        for gate in range(GATES):
-            spread = psum.tile([P, HID], F32, tag="bank")
-            nc.tensor.matmul(
-                out=spread[:], lhsT=ones[:], rhs=bias_rows[:, gate, :], start=True, stop=True
-            )
-            nc.scalar.copy(out=bias_all[:, gate, :], in_=spread[:])
-
         z_codes = resident.tile([P, BLOCKS, P], U32, align_bytes=64)
         z_planes = resident.tile([P, BLOCKS, P], U8, align_bytes=64)
+        values = resident.tile([P, GATES, ROW_TILES, HID], F32)
+        out_rows = out.rearrange("(p m) h -> p m h", m=ROW_TILES)
 
-        def quantise(load, grouped):
-            blocks = slice(load * LOAD_BLOCKS, (load + 1) * LOAD_BLOCKS)
-            nc.vector.quantize_mx(
-                out=z_codes[:, blocks, :].rearrange("p b r -> p (b r)").bitcast(FP8X4),
-                scales=z_planes[:, blocks, :].rearrange("p b r -> p (b r)"),
-                in_=grouped[:].rearrange("p b r t -> p (b r t)"),
-            )
+        def spread_biases():
+            for gate in range(GATES):
+                spread = psum.tile([P, HID], F32, tag="bank", name="spread")
+                nc.tensor.matmul(
+                    out=spread[:], lhsT=ones[:], rhs=bias_rows[:, gate, :], start=True, stop=True
+                )
+                nc.scalar.copy(out=bias_all[:, gate, :], in_=spread[:])
 
-        copied = None
-        for load in range(LOADS):
+        def turn(load):
             pair_words = z_raw[:, load, :].bitcast(F32)
-            grouped = stage.tile([P, LOAD_BLOCKS, P, PACK], BF16, align_bytes=64)
+            grouped = stage.tile([P, LOAD_BLOCKS, P, PACK], BF16, align_bytes=64, name="grouped")
             grouped_words = grouped[:].bitcast(F32)
             for half in range(2):
-                turned = psum.tile([P, 2, 2, P], F32, tag="bank")
+                turned = psum.tile([P, 2, 2, P], F32, tag="bank", name="turned")
                 for b in range(2):
                     first_word = (2 * half + b) * PAIR_WORDS
                     for u in range(2):
@@ -157,22 +181,31 @@ def tile_rnn_unit_kernel(
                     nc.scalar.copy(out=grouped_words[:, 0:2, :, :], in_=side_by_side)
                 else:
                     nc.vector.tensor_copy(out=grouped_words[:, 2:4, :, :], in_=side_by_side)
-            if copied is not None:
-                quantise(*copied)
-            copied = (load, grouped)
-        quantise(*copied)
+            return grouped
 
-        values = resident.tile([P, GATES, ROW_TILES, HID], F32)
-        out_rows = out.rearrange("(p m) h -> p m h", m=ROW_TILES)
+        def quantise(load, grouped):
+            blocks = slice(load * LOAD_BLOCKS, (load + 1) * LOAD_BLOCKS)
+            nc.vector.quantize_mx(
+                out=z_codes[:, blocks, :].rearrange("p b r -> p (b r)").bitcast(FP8X4),
+                scales=z_planes[:, blocks, :].rearrange("p b r -> p (b r)"),
+                in_=grouped[:].rearrange("p b r t -> p (b r t)"),
+            )
 
-        def project(gate, pair, first, width):
+        def prepare(pair):
+            first = turn(2 * pair)
+            second = turn(2 * pair + 1)
+            quantise(2 * pair, first)
+            quantise(2 * pair + 1, second)
+
+        def project(gate, tiles, first, width):
             cols = slice(first, first + width)
             sums = [
-                psum.tile([P, width], F32, tag="bank", name="sums%d" % i) for i in range(PAIR)
+                psum.tile([P, width], F32, tag="bank", name="sums%d" % i)
+                for i in range(len(tiles))
             ]
             for g in range(PASSES):
-                for i in range(PAIR):
-                    block = block_of[(PAIR * pair + i, g)]
+                for i, m in enumerate(tiles):
+                    block = block_of(m, g)
                     nc.tensor.matmul_mx(
                         out=sums[i][:],
                         lhsT=z_codes[:, block, :].bitcast(FP8X4),
@@ -182,8 +215,8 @@ def tile_rnn_unit_kernel(
                         start=(g == 0),
                         stop=(g == PASSES - 1),
                     )
-            for i in range(PAIR):
-                gate_rows = values[:, gate, PAIR * pair + i, cols]
+            for i, m in enumerate(tiles):
+                gate_rows = values[:, gate, m, cols]
                 nc.vector.tensor_add(out=gate_rows, in0=sums[i][:], in1=bias_all[:, gate, cols])
                 nc.scalar.activation(out=gate_rows, in_=gate_rows, func=gates[gate][3])
 
@@ -219,16 +252,27 @@ def tile_rnn_unit_kernel(
                     )
                     nc.sync.dma_start(out=out_rows[:, m, cols], in_=values[:, OUTPUT, m, cols])
 
-        steps = [(FORGET, pair, 0, HID) for pair in range(PAIRS)]
+        projected = []
+
+        def step(gate, pair, first, width):
+            project(gate, (PAIR * pair, PAIR * pair + 1), first, width)
+            if projected:
+                combine(*projected[0])
+                projected.clear()
+            projected.append((gate, pair, first, width))
+
+        prepare(0)
+        spread_biases()
         for pair in range(PAIRS):
-            steps.extend([(CANDIDATE, pair, 0, HID), (INPUT, pair, 0, HID)])
-        steps.extend([(OUTPUT, pair, 0, HID) for pair in range(PAIRS - 1)])
+            if pair + 1 < PAIRS:
+                prepare(pair + 1)
+            step(FORGET, pair, 0, HID)
+        for pair in range(PAIRS):
+            step(CANDIDATE, pair, 0, HID)
+            step(INPUT, pair, 0, HID)
+        for pair in range(PAIRS - 1):
+            step(OUTPUT, pair, 0, HID)
         half = HID // 2
-        steps.extend([(OUTPUT, PAIRS - 1, first, half) for first in (0, half)])
-        projected = None
-        for step in steps:
-            project(*step)
-            if projected is not None:
-                combine(*projected)
-            projected = step
-        combine(*projected)
+        for first in (0, half):
+            step(OUTPUT, PAIRS - 1, first, half)
+        combine(*projected[0])

@@ -28,6 +28,7 @@ PAIR_WORDS = K_PASS // 2
 
 FORGET, CANDIDATE, INPUT, OUTPUT = 0, 1, 2, 3
 GATES = 4
+LATE = 2
 
 FLOPS = 2 * BATCH * K * GATES * HID
 
@@ -256,9 +257,9 @@ def tile_rnn_unit_kernel(
 
         def step(gate, pair, first, width):
             project(gate, (PAIR * pair, PAIR * pair + 1), first, width)
-            if projected:
+            if len(projected) == LATE:
                 combine(*projected[0])
-                projected.clear()
+                projected.remove(projected[0])
             projected.append((gate, pair, first, width))
 
         prepare(0)
@@ -275,4 +276,5 @@ def tile_rnn_unit_kernel(
         half = HID // 2
         for first in (0, half):
             step(OUTPUT, PAIRS - 1, first, half)
-        combine(*projected[0])
+        for waiting in projected:
+            combine(*waiting)

@@ -29,6 +29,9 @@ PAIR_WORDS = K_PASS // 2
 FORGET, CANDIDATE, INPUT, OUTPUT = 0, 1, 2, 3
 GATES = 4
 LATE = 2
+W_PLANE_SKIP = 64
+Z_CODE_SKIP = 32
+Z_PLANE_SKIP = 192
 
 FLOPS = 2 * BATCH * K * GATES * HID
 
@@ -86,14 +89,15 @@ def tile_rnn_unit_kernel(
         nc.vector.memset(ones[:], 1.0)
         warm = resident.tile([P, 1], F32)
         nc.scalar.activation(out=warm[:], in_=ones[:, 0:1], func=ACT.Sigmoid)
-        w_planes = resident.tile([P, GATES, HID], U8, align_bytes=64)
-        nc.vector.memset(w_planes[:].rearrange("p w n -> p (w n)").bitcast(I32), 0)
+        w_planes_tile = resident.tile([P, W_PLANE_SKIP + GATES * HID], U8, align_bytes=256)
+        nc.vector.memset(w_planes_tile[:].bitcast(I32), 0)
+        w_planes = w_planes_tile[:, W_PLANE_SKIP:].rearrange("p (w n) -> p w n", w=GATES)
         nc.vector.tensor_copy(out=bias_rows[0:1, :, :], in_=bias_line[:])
         identity = resident.tile([P, P], F32)
         make_identity(nc, identity[:])
 
         z_raw = resident.tile([P, LOADS, LOAD_BLOCKS * K_PASS], BF16)
-        w_words = resident.tile([P, GATES, PASSES, HID], I32, align_bytes=64)
+        w_words = resident.tile([P, GATES, PASSES, HID], I32, align_bytes=256)
         old_rows = resident.tile([P, ROW_TILES, HID], BF16)
         x_flat = input_x.rearrange("(p m) k -> p (m k)", m=ROW_TILES)
         time_flat = previous_time.rearrange("(p m) k -> p (m k)", m=ROW_TILES)
@@ -150,8 +154,10 @@ def tile_rnn_unit_kernel(
         load_weight(OUTPUT)
 
         bias_all = resident.tile([P, GATES, HID], F32)
-        z_codes = resident.tile([P, BLOCKS, P], U32, align_bytes=64)
-        z_planes = resident.tile([P, BLOCKS, P], U8, align_bytes=64)
+        z_codes_tile = resident.tile([P, Z_CODE_SKIP + BLOCKS * P], U32, align_bytes=256)
+        z_codes = z_codes_tile[:, Z_CODE_SKIP:].rearrange("p (b r) -> p b r", b=BLOCKS)
+        z_planes_tile = resident.tile([P, Z_PLANE_SKIP + BLOCKS * P], U8, align_bytes=256)
+        z_planes = z_planes_tile[:, Z_PLANE_SKIP:].rearrange("p (b r) -> p b r", b=BLOCKS)
         values = resident.tile([P, GATES, ROW_TILES, HID], F32)
         out_rows = out.rearrange("(p m) h -> p m h", m=ROW_TILES)
 

@@ -210,18 +210,21 @@ def tile_rnn_unit_kernel(
                 psum.tile([P, width], F32, tag="bank", name="sums%d" % i)
                 for i in range(len(tiles))
             ]
-            for g in range(PASSES):
-                for i, m in enumerate(tiles):
-                    block = block_of(m, g)
-                    nc.tensor.matmul_mx(
-                        out=sums[i][:],
-                        lhsT=z_codes[:, block, :].bitcast(FP8X4),
-                        lhsT_scale=z_planes[:, block, :],
-                        rhs=w_words[:, gate, g, cols].bitcast(FP8X4),
-                        rhs_scale=w_planes[PACK * g : P, gate, cols],
-                        start=(g == 0),
-                        stop=(g == PASSES - 1),
-                    )
+            if gate == OUTPUT:
+                order = [(g, i) for i in range(len(tiles)) for g in range(PASSES)]
+            else:
+                order = [(g, i) for g in range(PASSES) for i in range(len(tiles))]
+            for g, i in order:
+                block = block_of(tiles[i], g)
+                nc.tensor.matmul_mx(
+                    out=sums[i][:],
+                    lhsT=z_codes[:, block, :].bitcast(FP8X4),
+                    lhsT_scale=z_planes[:, block, :],
+                    rhs=w_words[:, gate, g, cols].bitcast(FP8X4),
+                    rhs_scale=w_planes[PACK * g : P, gate, cols],
+                    start=(g == 0),
+                    stop=(g == PASSES - 1),
+                )
             for i, m in enumerate(tiles):
                 gate_rows = values[:, gate, m, cols]
                 nc.vector.tensor_add(out=gate_rows, in0=sums[i][:], in1=bias_all[:, gate, cols])
@@ -229,7 +232,10 @@ def tile_rnn_unit_kernel(
 
         def combine(gate, pair, first, width):
             cols = slice(first, first + width)
-            for i, engine in enumerate((nc.gpsimd, nc.vector)):
+            engines = (nc.gpsimd, nc.vector)
+            if gate == OUTPUT and pair == PAIRS - 1:
+                engines = (nc.vector, nc.vector)
+            for i, engine in enumerate(engines):
                 m = PAIR * pair + i
                 if gate == FORGET:
                     engine.tensor_mul(

@@ -83,10 +83,12 @@ def tile_rnn_unit_kernel(
                 out=bias_line[0:1, gate, :],
                 in_=gates[gate][2].rearrange("(o n) -> o n", o=1),
             )
-        bias_rows = resident.tile([P, GATES, HID], BF16)
-        nc.vector.memset(bias_rows[:].rearrange("p w n -> p (w n)").bitcast(I32), 0)
         ones = resident.tile([P, P], BF16)
         nc.vector.memset(ones[:], 1.0)
+        idle_rows = resident.tile([P, HID], BF16)
+        nc.vector.memset(idle_rows[:], 0.0)
+        bias_rows = resident.tile([P, GATES, HID], BF16)
+        nc.vector.memset(bias_rows[:].rearrange("p w n -> p (w n)").bitcast(I32), 0)
         warm = resident.tile([P, 1], F32)
         nc.scalar.activation(out=warm[:], in_=ones[:, 0:1], func=ACT.Sigmoid)
         w_planes_tile = resident.tile([P, W_PLANE_SKIP + GATES * HID], U8, align_bytes=256)
@@ -161,6 +163,13 @@ def tile_rnn_unit_kernel(
         values = resident.tile([P, GATES, ROW_TILES, HID], F32)
         out_rows = out.rearrange("(p m) h -> p m h", m=ROW_TILES)
 
+        def keep_busy(count):
+            unread = psum.tile([P, HID], F32, tag="bank", name="unread")
+            for n in range(count):
+                nc.tensor.matmul(
+                    out=unread[:], lhsT=ones[:], rhs=idle_rows[:], start=True, stop=True
+                )
+
         def spread_biases():
             for gate in range(GATES):
                 spread = psum.tile([P, HID], F32, tag="bank", name="spread")
@@ -198,8 +207,10 @@ def tile_rnn_unit_kernel(
                 in_=grouped[:].rearrange("p b r t -> p (b r t)"),
             )
 
-        def prepare(pair):
+        def prepare(pair, busy):
             first = turn(2 * pair)
+            if busy:
+                keep_busy(busy)
             second = turn(2 * pair + 1)
             quantise(2 * pair, first)
             quantise(2 * pair + 1, second)
@@ -274,11 +285,13 @@ def tile_rnn_unit_kernel(
                 projected.remove(projected[0])
             projected.append((gate, pair, first, width))
 
-        prepare(0)
+        keep_busy(4)
+        prepare(0, 2)
         spread_biases()
+        prepare(1, 2)
         for pair in range(PAIRS):
-            if pair + 1 < PAIRS:
-                prepare(pair + 1)
+            if 0 < pair < PAIRS - 1:
+                prepare(pair + 1, 0)
             step(FORGET, pair, 0, HID)
         for pair in range(PAIRS):
             step(CANDIDATE, pair, 0, HID)

@@ -28,7 +28,6 @@ PAIR_WORDS = K_PASS // 2
 
 FORGET, CANDIDATE, INPUT, OUTPUT = 0, 1, 2, 3
 GATES = 4
-LATE = 2
 W_PLANE_SKIP = 64
 Z_CODE_SKIP = 32
 Z_PLANE_SKIP = 192
@@ -170,8 +169,8 @@ def tile_rnn_unit_kernel(
                     out=unread[:], lhsT=ones[:], rhs=idle_rows[:], start=True, stop=True
                 )
 
-        def spread_biases():
-            for gate in range(GATES):
+        def spread_biases(gates_now):
+            for gate in gates_now:
                 spread = psum.tile([P, HID], F32, tag="bank", name="spread")
                 nc.tensor.matmul(
                     out=spread[:], lhsT=ones[:], rhs=bias_rows[:, gate, :], start=True, stop=True
@@ -193,10 +192,11 @@ def tile_rnn_unit_kernel(
                             identity[:],
                         )
                 side_by_side = turned[:].rearrange("p b u r -> p b r u")
-                if half == 0:
-                    nc.scalar.copy(out=grouped_words[:, 0:2, :, :], in_=side_by_side)
+                target = grouped_words[:, 2 * half : 2 * half + 2, :, :]
+                if half == 1:
+                    nc.vector.tensor_copy(out=target, in_=side_by_side)
                 else:
-                    nc.vector.tensor_copy(out=grouped_words[:, 2:4, :, :], in_=side_by_side)
+                    nc.scalar.copy(out=target, in_=side_by_side)
             return grouped
 
         def quantise(load, grouped):
@@ -207,10 +207,10 @@ def tile_rnn_unit_kernel(
                 in_=grouped[:].rearrange("p b r t -> p (b r t)"),
             )
 
-        def prepare(pair, busy):
+        def prepare(pair, between=None):
             first = turn(2 * pair)
-            if busy:
-                keep_busy(busy)
+            if between:
+                spread_biases(between)
             second = turn(2 * pair + 1)
             quantise(2 * pair, first)
             quantise(2 * pair + 1, second)
@@ -241,65 +241,75 @@ def tile_rnn_unit_kernel(
                 nc.vector.tensor_add(out=gate_rows, in0=sums[i][:], in1=bias_all[:, gate, cols])
                 nc.scalar.activation(out=gate_rows, in_=gate_rows, func=gates[gate][3])
 
-        def combine(gate, pair, first, width):
-            cols = slice(first, first + width)
-            engines = (nc.gpsimd, nc.vector)
-            if gate == OUTPUT and pair == PAIRS - 1:
-                engines = (nc.vector, nc.vector)
-            for i, engine in enumerate(engines):
-                m = PAIR * pair + i
-                if gate == FORGET:
-                    engine.tensor_mul(
-                        out=values[:, FORGET, m, cols],
-                        in0=values[:, FORGET, m, cols],
-                        in1=old_rows[:, m, cols],
-                    )
-                if gate == INPUT:
-                    engine.tensor_mul(
-                        out=values[:, INPUT, m, cols],
-                        in0=values[:, INPUT, m, cols],
-                        in1=values[:, CANDIDATE, m, cols],
-                    )
-                    engine.tensor_add(
-                        out=values[:, INPUT, m, cols],
-                        in0=values[:, INPUT, m, cols],
-                        in1=values[:, FORGET, m, cols],
-                    )
-                    nc.scalar.activation(
-                        out=values[:, INPUT, m, cols], in_=values[:, INPUT, m, cols], func=ACT.Tanh
-                    )
-                if gate == OUTPUT:
-                    engine.tensor_mul(
-                        out=values[:, OUTPUT, m, cols],
-                        in0=values[:, OUTPUT, m, cols],
-                        in1=values[:, INPUT, m, cols],
-                    )
-                    nc.sync.dma_start(out=out_rows[:, m, cols], in_=values[:, OUTPUT, m, cols])
+        def shared(pair):
+            return ((PAIR * pair, nc.gpsimd), (PAIR * pair + 1, nc.vector))
 
-        projected = []
+        def product(engine, gate, other, m, cols):
+            engine.tensor_mul(
+                out=values[:, gate, m, cols], in0=values[:, gate, m, cols], in1=other
+            )
+
+        def forget_old(pair, cols):
+            for m, engine in shared(pair):
+                product(engine, FORGET, old_rows[:, m, cols], m, cols)
+
+        def input_candidate(pair, cols):
+            for m, engine in shared(pair):
+                product(engine, INPUT, values[:, CANDIDATE, m, cols], m, cols)
+
+        def new_state(pair, cols):
+            for m, engine in shared(pair):
+                state = values[:, INPUT, m, cols]
+                engine.tensor_add(out=state, in0=state, in1=values[:, FORGET, m, cols])
+                nc.scalar.activation(out=state, in_=state, func=ACT.Tanh)
+
+        def hidden(pair, cols):
+            for m in (PAIR * pair, PAIR * pair + 1):
+                product(nc.vector, OUTPUT, values[:, INPUT, m, cols], m, cols)
+                nc.sync.dma_start(out=out_rows[:, m, cols], in_=values[:, OUTPUT, m, cols])
+
+        followers = {
+            FORGET: ((1, forget_old),),
+            CANDIDATE: (),
+            INPUT: ((2, input_candidate), (3, new_state)),
+            OUTPUT: ((1, hidden),),
+        }
+        waiting = []
+
+        def follow():
+            for entry in list(waiting):
+                entry[0] -= 1
+                if entry[0] == 0:
+                    entry[1](entry[2], entry[3])
+                    waiting.remove(entry)
 
         def step(gate, pair, first, width):
             project(gate, (PAIR * pair, PAIR * pair + 1), first, width)
-            if len(projected) == LATE:
-                combine(*projected[0])
-                projected.remove(projected[0])
-            projected.append((gate, pair, first, width))
+            follow()
+            for steps, work in followers[gate]:
+                waiting.append([steps, work, pair, slice(first, first + width)])
 
         keep_busy(4)
-        prepare(0, 2)
-        spread_biases()
-        prepare(1, 2)
-        for pair in range(PAIRS):
-            if 0 < pair < PAIRS - 1:
-                prepare(pair + 1, 0)
-            step(FORGET, pair, 0, HID)
-        for pair in range(PAIRS):
-            step(CANDIDATE, pair, 0, HID)
-            step(INPUT, pair, 0, HID)
-        for pair in range(PAIRS - 1):
-            step(OUTPUT, pair, 0, HID)
-        half = HID // 2
-        for first in (0, half):
-            step(OUTPUT, PAIRS - 1, first, half)
-        for waiting in projected:
-            combine(*waiting)
+        prepare(0, (FORGET, CANDIDATE,))
+        prepare(1, (INPUT, OUTPUT,))
+        step(FORGET, 0, 0, HID)
+        prepare(2)
+        step(FORGET, 1, 0, HID)
+        prepare(3)
+        step(FORGET, 2, 0, HID)
+        step(FORGET, 3, 0, HID)
+        step(INPUT, 0, 0, HID)
+        step(CANDIDATE, 0, 0, HID)
+        step(INPUT, 1, 0, HID)
+        step(CANDIDATE, 1, 0, HID)
+        step(INPUT, 2, 0, HID)
+        step(CANDIDATE, 2, 0, HID)
+        step(INPUT, 3, 0, HID)
+        step(CANDIDATE, 3, 0, HID)
+        step(OUTPUT, 0, 0, HID)
+        step(OUTPUT, 1, 0, HID)
+        step(OUTPUT, 2, 0, HID)
+        for first in (0, HID // 2):
+            step(OUTPUT, PAIRS - 1, first, HID // 2)
+        while waiting:
+            follow()

@@ -150,8 +150,8 @@ def tile_rnn_unit_kernel(
         load_old(1)
         load_old(2)
         load_old(3)
-        load_weight(CANDIDATE)
         load_weight(INPUT)
+        load_weight(CANDIDATE)
         load_weight(OUTPUT)
 
         bias_all = resident.tile([P, GATES, HID], F32)
@@ -289,8 +289,9 @@ def tile_rnn_unit_kernel(
             for steps, work in followers[gate]:
                 waiting.append([steps, work, pair, slice(first, first + width)])
 
-        keep_busy(4)
+        keep_busy(8)
         prepare(0, (FORGET, CANDIDATE,))
+        keep_busy(2)
         prepare(1, (INPUT, OUTPUT,))
         step(FORGET, 0, 0, HID)
         prepare(2)

import concourse.mybir as mybir
from concourse.masks import make_identity

F32 = mybir.dt.float32
BF16 = mybir.dt.bfloat16
I32 = mybir.dt.int32
U32 = mybir.dt.uint32
U8 = mybir.dt.uint8
FP8X4 = mybir.dt.float8_e4m3fn_x4
ACT = mybir.ActivationFunctionType

P = 128
PACK = 4
K_PASS = P * PACK
BATCH = 1024
HID = 512
K = 2048
PASSES = K // K_PASS
ROW_TILES = BATCH // P
PAIR = 2
PAIRS = ROW_TILES // PAIR
BANKS = 8

BLOCKS = ROW_TILES * PASSES
LOAD_BLOCKS = 4
LOADS = BLOCKS // LOAD_BLOCKS
PAIR_WORDS = K_PASS // 2

FORGET, CANDIDATE, INPUT, OUTPUT = 0, 1, 2, 3
GATES = 4
W_PLANE_SKIP = 64
Z_CODE_SKIP = 32
Z_PLANE_SKIP = 192

FLOPS = 2 * BATCH * K * GATES * HID


def block_of(m, g):
    pair, i = m // PAIR, m % PAIR
    if g < 2:
        return LOAD_BLOCKS * (2 * pair) + 2 * i + g
    return LOAD_BLOCKS * (2 * pair + 1) + 2 * (g - 2) + i


def tile_rnn_unit_kernel(
    tc,
    input_x,
    previous_time,
    previous_layer,
    old_state,
    Wi_words,
    Wi_scales,
    bi,
    Wf_words,
    Wf_scales,
    bf,
    Wo_words,
    Wo_scales,
    bo,
    Ws_words,
    Ws_scales,
    bs_state,
    out,
):
    nc = tc.nc
    gates = (
        (Wf_words, Wf_scales, bf, ACT.Sigmoid),
        (Ws_words, Ws_scales, bs_state, ACT.Tanh),
        (Wi_words, Wi_scales, bi, ACT.Sigmoid),
        (Wo_words, Wo_scales, bo, ACT.Sigmoid),
    )

    with (
        tc.tile_pool(name="resident", bufs=1) as resident,
        tc.tile_pool(name="stage", bufs=3) as stage,
        tc.psum_pool(name="psum", bufs=BANKS) as psum,
        tc.manual_schedule(),
    ):
        bias_line = resident.tile([1, GATES, HID], BF16)
        for gate in range(GATES):
            nc.sync.dma_start(
                out=bias_line[0:1, gate, :],
                in_=gates[gate][2].rearrange("(o n) -> o n", o=1),
            )
        ones = resident.tile([P, P], BF16)
        nc.vector.memset(ones[:], 1.0)
        idle_rows = resident.tile([P, HID], BF16)
        nc.vector.memset(idle_rows[:], 0.0)
        bias_rows = resident.tile([P, GATES, HID], BF16)
        nc.vector.memset(bias_rows[:].rearrange("p w n -> p (w n)").bitcast(I32), 0)
        warm = resident.tile([P, 1], F32)
        nc.scalar.activation(out=warm[:], in_=ones[:, 0:1], func=ACT.Sigmoid)
        w_planes_tile = resident.tile([P, W_PLANE_SKIP + GATES * HID], U8, align_bytes=256)
        nc.vector.memset(w_planes_tile[:].bitcast(I32), 0)
        w_planes = w_planes_tile[:, W_PLANE_SKIP:].rearrange("p (w n) -> p w n", w=GATES)
        nc.vector.tensor_copy(out=bias_rows[0:1, :, :], in_=bias_line[:])
        identity = resident.tile([P, P], F32)
        make_identity(nc, identity[:])

        z_raw = resident.tile([P, LOADS, LOAD_BLOCKS * K_PASS], BF16)
        w_words = resident.tile([P, GATES, PASSES, HID], I32, align_bytes=256)
        old_rows = resident.tile([P, ROW_TILES, HID], BF16)
        x_flat = input_x.rearrange("(p m) k -> p (m k)", m=ROW_TILES)
        time_flat = previous_time.rearrange("(p m) k -> p (m k)", m=ROW_TILES)
        layer_flat = previous_layer.rearrange("(p m) k -> p (m k)", m=ROW_TILES)
        old_view = old_state.rearrange("(p m) h -> p m h", m=ROW_TILES)

        def load_z(pair, pieces):
            width = LOAD_BLOCKS * K_PASS // pieces
            for piece in range(pieces):
                nc.sync.dma_start(
                    out=z_raw[:, 2 * pair, piece * width : (piece + 1) * width],
                    in_=x_flat[
                        :,
                        pair * LOAD_BLOCKS * K_PASS
                        + piece * width : pair * LOAD_BLOCKS * K_PASS
                        + (piece + 1) * width,
                    ],
                )
            half = PAIR * K_PASS
            for n, flat in enumerate((time_flat, layer_flat)):
                nc.sync.dma_start(
                    out=z_raw[:, 2 * pair + 1, n * half : (n + 1) * half],
                    in_=flat[:, pair * half : (pair + 1) * half],
                )

        def load_weight(gate):
            words, scales = gates[gate][0], gates[gate][1]
            for quadrant in range(4):
                nc.sync.dma_start(
                    out=w_planes[32 * quadrant : 32 * quadrant + 16, gate, :].bitcast(I32),
                    in_=scales[:, 4 * quadrant : 4 * quadrant + 4, :].bitcast(I32),
                )
            for g in range(PASSES):
                nc.sync.dma_start(
                    out=w_words[:, gate, g, :],
                    in_=words[g].rearrange("p n t -> p (n t)").bitcast(I32),
                )

        def load_old(pair):
            rows = slice(PAIR * pair, PAIR * (pair + 1))
            nc.sync.dma_start(out=old_rows[:, rows, :], in_=old_view[:, rows, :])

        load_z(0, 2)
        load_z(1, 1)
        load_weight(FORGET)
        load_z(2, 1)
        load_old(0)
        load_z(3, 1)
        load_old(1)
        load_old(2)
        load_old(3)
        load_weight(INPUT)
        load_weight(CANDIDATE)
        load_weight(OUTPUT)

        bias_all = resident.tile([P, GATES, HID], F32)
        z_codes_tile = resident.tile([P, Z_CODE_SKIP + BLOCKS * P], U32, align_bytes=256)
        z_codes = z_codes_tile[:, Z_CODE_SKIP:].rearrange("p (b r) -> p b r", b=BLOCKS)
        z_planes_tile = resident.tile([P, Z_PLANE_SKIP + BLOCKS * P], U8, align_bytes=256)
        z_planes = z_planes_tile[:, Z_PLANE_SKIP:].rearrange("p (b r) -> p b r", b=BLOCKS)
        values = resident.tile([P, GATES, ROW_TILES, HID], F32)
        out_rows = out.rearrange("(p m) h -> p m h", m=ROW_TILES)

        def keep_busy(count):
            unread = psum.tile([P, HID], F32, tag="bank", name="unread")
            for n in range(count):
                nc.tensor.matmul(
                    out=unread[:], lhsT=ones[:], rhs=idle_rows[:], start=True, stop=True
                )

        def spread_biases(gates_now):
            for gate in gates_now:
                spread = psum.tile([P, HID], F32, tag="bank", name="spread")
                nc.tensor.matmul(
                    out=spread[:], lhsT=ones[:], rhs=bias_rows[:, gate, :], start=True, stop=True
                )
                nc.scalar.copy(out=bias_all[:, gate, :], in_=spread[:])

        def turn(load):
            pair_words = z_raw[:, load, :].bitcast(F32)
            grouped = stage.tile([P, LOAD_BLOCKS, P, PACK], BF16, align_bytes=64, name="grouped")
            grouped_words = grouped[:].bitcast(F32)
            for half in range(2):
                turned = psum.tile([P, 2, 2, P], F32, tag="bank", name="turned")
                for b in range(2):
                    first_word = (2 * half + b) * PAIR_WORDS
                    for u in range(2):
                        nc.tensor.transpose(
                            turned[:, b, u, :],
                            pair_words[:, first_word + u : first_word + PAIR_WORDS : 2],
                            identity[:],
                        )
                side_by_side = turned[:].rearrange("p b u r -> p b r u")
                target = grouped_words[:, 2 * half : 2 * half + 2, :, :]
                if half == 1:
                    nc.vector.tensor_copy(out=target, in_=side_by_side)
                else:
                    nc.scalar.copy(out=target, in_=side_by_side)
            return grouped

        def quantise(load, grouped):
            blocks = slice(load * LOAD_BLOCKS, (load + 1) * LOAD_BLOCKS)
            nc.vector.quantize_mx(
                out=z_codes[:, blocks, :].rearrange("p b r -> p (b r)").bitcast(FP8X4),
                scales=z_planes[:, blocks, :].rearrange("p b r -> p (b r)"),
                in_=grouped[:].rearrange("p b r t -> p (b r t)"),
            )

        def prepare(pair, between=None):
            first = turn(2 * pair)
            if between:
                spread_biases(between)
            second = turn(2 * pair + 1)
            quantise(2 * pair, first)
            quantise(2 * pair + 1, second)

        def project(gate, tiles, first, width):
            cols = slice(first, first + width)
            sums = [
                psum.tile([P, width], F32, tag="bank", name="sums%d" % i)
                for i in range(len(tiles))
            ]
            if gate == OUTPUT:
                order = [(g, i) for i in range(len(tiles)) for g in range(PASSES)]
            else:
                order = [(g, i) for g in range(PASSES) for i in range(len(tiles))]
            for g, i in order:
                block = block_of(tiles[i], g)
                nc.tensor.matmul_mx(
                    out=sums[i][:],
                    lhsT=z_codes[:, block, :].bitcast(FP8X4),
                    lhsT_scale=z_planes[:, block, :],
                    rhs=w_words[:, gate, g, cols].bitcast(FP8X4),
                    rhs_scale=w_planes[PACK * g : P, gate, cols],
                    start=(g == 0),
                    stop=(g == PASSES - 1),
                )
            for i, m in enumerate(tiles):
                gate_rows = values[:, gate, m, cols]
                nc.vector.tensor_add(out=gate_rows, in0=sums[i][:], in1=bias_all[:, gate, cols])
                nc.scalar.activation(out=gate_rows, in_=gate_rows, func=gates[gate][3])

        def shared(pair):
            return ((PAIR * pair, nc.gpsimd), (PAIR * pair + 1, nc.vector))

        def product(engine, gate, other, m, cols):
            engine.tensor_mul(
                out=values[:, gate, m, cols], in0=values[:, gate, m, cols], in1=other
            )

        def forget_old(pair, cols):
            for m, engine in shared(pair):
                product(engine, FORGET, old_rows[:, m, cols], m, cols)

        def input_candidate(pair, cols):
            for m, engine in shared(pair):
                product(engine, INPUT, values[:, CANDIDATE, m, cols], m, cols)

        def new_state(pair, cols):
            for m, engine in shared(pair):
                state = values[:, INPUT, m, cols]
                engine.tensor_add(out=state, in0=state, in1=values[:, FORGET, m, cols])
                nc.scalar.activation(out=state, in_=state, func=ACT.Tanh)

        def hidden(pair, cols):
            for m in (PAIR * pair, PAIR * pair + 1):
                product(nc.vector, OUTPUT, values[:, INPUT, m, cols], m, cols)
                nc.sync.dma_start(out=out_rows[:, m, cols], in_=values[:, OUTPUT, m, cols])

        followers = {
            FORGET: ((1, forget_old),),
            CANDIDATE: (),
            INPUT: ((2, input_candidate), (3, new_state)),
            OUTPUT: ((1, hidden),),
        }
        waiting = []

        def follow():
            for entry in list(waiting):
                entry[0] -= 1
                if entry[0] == 0:
                    entry[1](entry[2], entry[3])
                    waiting.remove(entry)

        def step(gate, pair, first, width):
            project(gate, (PAIR * pair, PAIR * pair + 1), first, width)
            follow()
            for steps, work in followers[gate]:
                waiting.append([steps, work, pair, slice(first, first + width)])

        keep_busy(8)
        prepare(0, (FORGET, CANDIDATE,))
        keep_busy(2)
        prepare(1, (INPUT, OUTPUT,))
        step(FORGET, 0, 0, HID)
        prepare(2)
        step(FORGET, 1, 0, HID)
        prepare(3)
        step(FORGET, 2, 0, HID)
        step(FORGET, 3, 0, HID)
        step(INPUT, 0, 0, HID)
        step(CANDIDATE, 0, 0, HID)
        step(INPUT, 1, 0, HID)
        step(CANDIDATE, 1, 0, HID)
        step(INPUT, 2, 0, HID)
        step(CANDIDATE, 2, 0, HID)
        step(INPUT, 3, 0, HID)
        step(CANDIDATE, 3, 0, HID)
        step(OUTPUT, 0, 0, HID)
        step(OUTPUT, 1, 0, HID)
        step(OUTPUT, 2, 0, HID)
        for first in (0, HID // 2):
            step(OUTPUT, PAIRS - 1, first, HID // 2)
        while waiting:
            follow()
